import numpy as np
import ml_dtypes


def mxq(x, axis, fmt="e4m3"):
    dtype, down = {"e4m3": (ml_dtypes.float8_e4m3fn, 7), "e5m2": (ml_dtypes.float8_e5m2, 14)}[fmt]
    v = np.moveaxis(np.asarray(x, np.float32).astype(ml_dtypes.bfloat16).astype(np.float64), axis, -1)
    blocks = v.reshape(v.shape[:-1] + (-1, 32))
    amax = np.abs(blocks).max(-1, keepdims=True)
    byte = np.maximum(np.where(amax > 0, np.frexp(amax)[1] - 1 + 127, 0) - down, 1)
    scale = np.exp2(byte - 127.0)
    codes = (blocks / scale).astype(np.float32).astype(dtype).astype(np.float64)
    return np.moveaxis((codes * scale).reshape(v.shape), -1, axis)


WIDE = False


def mx_kscale(k):
    if not WIDE:
        return np.ones(k)
    levels = np.array([10, -10, 5, -5, 0])
    if k % 512:
        return np.exp2(np.random.permutation(np.resize(levels, k // 32))).repeat(32)
    a = np.empty((k // 512, 16))
    for p in range(k // 512):
        a[p, :8] = np.random.permutation(np.resize(levels, 8))
        for g in range(8):
            far = levels[np.abs(levels - a[p, g]) >= 10]
            a[p, g + 8] = far[np.random.randint(len(far))]
    return np.exp2(a.ravel()).repeat(32)


BF16 = ml_dtypes.bfloat16


def bf(x):
    return np.asarray(x, np.float32).astype(BF16)


def f64(x):
    return np.asarray(x).astype(np.float64)


B, N1, N2, D, H, FF = 2, 128, 256, 1024, 16, 4096
T = B * (N1 + N2)
EPS = 1e-5


def layer_norm(x, g, b):
    m = x.mean(-1, keepdims=True)
    v = ((x - m) * (x - m)).mean(-1, keepdims=True)
    return (x - m) * (1.0 / np.sqrt(v + EPS)) * g + b


def erf(z):
    a = np.minimum(np.abs(z), 6.0)
    a2 = a * a
    term, tot, n = a.copy(), a.copy(), 1.5
    while np.any(term > 1e-17 * tot):
        term = term * a2 / n
        tot = tot + term
        n += 1.0
    return np.sign(z) * tot * np.exp(-a2) / np.sqrt(0.25 * np.pi)


def gelu_erf(v):
    return 0.5 * v * (1.0 + erf(v * np.sqrt(0.5)))


def setup_inputs():
    s, t = mx_kscale(D), mx_kscale(D)
    return {"h_attn": bf(0.5 * np.random.standard_normal((T, D)) * s),
            "x": bf(np.random.standard_normal((T, D))),
            "w_proj": bf(np.random.standard_normal((D, D)) * 1.8 / np.sqrt(D) / s[:, None]),
            "b_proj": bf(0.1 * np.random.standard_normal(D)),
            "ls1": bf(0.6 + 0.2 * np.random.standard_normal(D)),
            "ln2_g": bf((1.0 + 0.1 * np.random.standard_normal(D)) * t),
            "ln2_b": bf(0.1 * np.random.standard_normal(D) * t),
            "w_fc1": bf(np.random.standard_normal((D, FF)) / np.sqrt(D) / t[:, None]),
            "b_fc1": bf(0.1 * np.random.standard_normal(FF))}


def reference(h_attn, x, w_proj, b_proj, ls1, ln2_g, ln2_b, w_fc1, b_fc1):
    p = (mxq(f64(h_attn), 1, "e4m3") @ mxq(f64(w_proj), 0, "e4m3")) + f64(b_proj)
    x_mid = f64(x) + f64(ls1) * p
    h2 = layer_norm(x_mid, f64(ln2_g), f64(ln2_b))
    u = (mxq(h2, 1, "e4m3") @ mxq(f64(w_fc1), 0, "e4m3")) + f64(b_fc1)
    return x_mid, gelu_erf(u)

@@ -1,0 +1,409 @@
+from contextlib import ExitStack
+
+import concourse.mybir as mybir
+from concourse.masks import make_identity
+
+F32 = mybir.dt.float32
+BF16 = mybir.dt.bfloat16
+U32 = mybir.dt.uint32
+U8 = mybir.dt.uint8
+FP8X4 = mybir.dt.float8_e4m3fn_x4
+ACT = mybir.ActivationFunctionType
+ALU = mybir.AluOpType
+
+P = 128
+PACK = 4
+K_PASS = P * PACK
+T, D, FF = 768, 1024, 4096
+PASSES = D // K_PASS
+TOK_TILES = T // P
+D_CHUNKS = D // P
+BANK = 512
+BLOCK = 2 * BANK
+FF_BLOCKS = FF // BLOCK
+UNITS_PER_BLOCK = PASSES * (BLOCK // BANK)
+TOKEN_GROUPS = ((0, 4), (4, 2))
+FIRST_GPSIMD_UNIT = 3 * UNITS_PER_BLOCK + 2
+STEPS_PER_GPSIMD_UNIT = 3
+EPS = 1e-5
+FLOPS = 2 * T * D * (D + FF)
+
+B_PROJ, LS1 = 0, D_CHUNKS
+LN_G, LN_B = 0, D_CHUNKS
+
+
+def tile_nestedtensorblock_pb_kernel(
+    tc, h_attn, x, w_proj, b_proj, ls1, ln2_g, ln2_b, w_fc1, b_fc1, out_0, out_1
+):
+    nc = tc.nc
+    with ExitStack() as ctx:
+        const = ctx.enter_context(tc.tile_pool(name="const", bufs=1))
+        tokens = ctx.enter_context(tc.tile_pool(name="tokens", bufs=1))
+        weights = ctx.enter_context(tc.tile_pool(name="weights", bufs=4))
+        stage = ctx.enter_context(tc.tile_pool(name="stage", bufs=4))
+        work = ctx.enter_context(tc.tile_pool(name="work", bufs=8))
+        psum = ctx.enter_context(tc.psum_pool(name="psum", bufs=1))
+
+        vec_rows = const.tile([P, P], BF16)
+        nc.vector.memset(vec_rows[:], 0.0)
+        for first_row, vec in ((B_PROJ, b_proj), (LS1, ls1)):
+            nc.scalar.dma_start(
+                out=vec_rows[first_row : first_row + D_CHUNKS, :],
+                in_=vec.rearrange("(r c) -> r c", c=P),
+            )
+        norm_rows = []
+        for i, vec in ((0, ln2_g), (1, ln2_b)):
+            rows = const.tile([P, PASSES, PACK], BF16, name="norm_rows%d" % i)
+            nc.scalar.dma_start(
+                out=rows[:], in_=vec.rearrange("(g p t) -> p g t", g=PASSES, t=PACK)
+            )
+            norm_rows.append(rows)
+
+        block_rows = {}
+        block_codes = {}
+        block_scales = {}
+
+        def new_block_rows(b):
+            block_rows[b] = weights.tile(
+                [P, PASSES, PACK, BLOCK], BF16, tag="w_rows", name="w_rows%d" % b
+            )
+
+        def new_block_codes(b):
+            block_codes[b] = weights.tile(
+                [P, PASSES * BLOCK], U32, tag="w_codes", name="w_codes%d" % b, align_bytes=64
+            )
+            block_scales[b] = weights.tile(
+                [P, PASSES * BLOCK], U8, tag="w_scales", name="w_scales%d" % b, align_bytes=64
+            )
+
+        new_block_rows(0)
+        wp_view = w_proj.rearrange("(g p t) n -> p g t n", g=PASSES, t=PACK)
+        for g in range(PASSES):
+            for u in range(2):
+                nc.sync.dma_start(
+                    out=block_rows[0][:, g, 2 * u : 2 * u + 2, :],
+                    in_=wp_view[:, g, 2 * u : 2 * u + 2, :],
+                )
+
+        h_rows = tokens.tile([P, TOK_TILES * D], BF16, tag="tok_a")
+        h_view = h_attn.rearrange("(p m) d -> p m d", p=P)
+        for pair in range(TOK_TILES // 2):
+            nc.sync.dma_start(
+                out=h_rows[:, 2 * D * pair : 2 * D * (pair + 1)].rearrange("p (m d) -> p m d", m=2),
+                in_=h_view[:, 2 * pair : 2 * pair + 2, :],
+            )
+
+        wf_view = w_fc1.rearrange("(g p t) n -> p g t n", g=PASSES, t=PACK)
+
+        def load_ff_block(b):
+            new_block_rows(b)
+            for g in range(PASSES):
+                nc.sync.dma_start(
+                    out=block_rows[b][:, g, :, :],
+                    in_=wf_view[:, g, :, BLOCK * (b - 1) : BLOCK * b],
+                )
+
+        load_ff_block(1)
+        x_rows = const.tile([P, TOK_TILES, D], BF16)
+        nc.sync.dma_start(out=x_rows[:], in_=x.rearrange("(p m) d -> p m d", p=P))
+        load_ff_block(2)
+        load_ff_block(3)
+
+        ident_f32 = const.tile([P, P], F32)
+        make_identity(nc, ident_f32[:])
+        ident_bf16 = const.tile([P, P], BF16)
+        nc.vector.tensor_copy(out=ident_bf16[:], in_=ident_f32[:])
+        neg_half = const.tile([P, 1], F32)
+        nc.vector.memset(neg_half[:], -0.5)
+        first_gelu = const.tile([P, 1], F32)
+        nc.scalar.activation(out=first_gelu[:], in_=neg_half[:], func=ACT.Gelu)
+
+        vec_cols = const.tile([P, 2 * D_CHUNKS], F32)
+        norm_cols = const.tile([P, 2 * D_CHUNKS], F32)
+        ls1_b = const.tile([P, D_CHUNKS], F32)
+
+        def transpose_vectors():
+            vec_ps = psum.tile([P, P], BF16, tag="turn", bufs=3)
+            nc.tensor.transpose(vec_ps[:], vec_rows[:], ident_bf16[:])
+            nc.vector.tensor_copy(out=vec_cols[:], in_=vec_ps[:, 0 : 2 * D_CHUNKS])
+            for i in range(2):
+                nc.vector.tensor_copy(
+                    out=norm_cols[:, D_CHUNKS * i : D_CHUNKS * (i + 1)],
+                    in_=norm_rows[i][:].rearrange("p g t -> p (g t)"),
+                )
+            nc.vector.tensor_mul(
+                ls1_b[:], vec_cols[:, LS1 : LS1 + D_CHUNKS], vec_cols[:, B_PROJ : B_PROJ + D_CHUNKS]
+            )
+
+        for b in range(4):
+            new_block_codes(b)
+        grouped_units = {}
+
+        def regroup_unit(u, copy):
+            b, g, half = u // UNITS_PER_BLOCK, (u % UNITS_PER_BLOCK) // 2, u % 2
+            grouped = stage.tile(
+                [P, BANK * PACK], BF16, tag="grouped", name="grouped%d" % u, align_bytes=64
+            )
+            copy(
+                out=grouped[:].rearrange("p (c i t) -> p c t i", i=4, t=PACK),
+                in_=block_rows[b][:, g, :, BANK * half : BANK * (half + 1)].rearrange(
+                    "p t (c i) -> p c t i", i=4
+                ),
+            )
+            grouped_units[u] = grouped[:]
+
+        def quantise_unit(u):
+            b, g, half = u // UNITS_PER_BLOCK, (u % UNITS_PER_BLOCK) // 2, u % 2
+            first = BLOCK * g + BANK * half
+            nc.vector.quantize_mx(
+                out=block_codes[b][:, first : first + BANK].bitcast(FP8X4),
+                scales=block_scales[b][:, first : first + BANK],
+                in_=grouped_units[u],
+            )
+
+        regroup_unit(0, nc.vector.tensor_copy)
+        regroup_unit(1, nc.scalar.copy)
+        quantise_unit(0)
+        regroup_unit(2, nc.vector.tensor_copy)
+        regroup_unit(3, nc.scalar.copy)
+        quantise_unit(1)
+        quantise_unit(2)
+        quantise_unit(3)
+        load_ff_block(4)
+        bias_fc1 = const.tile([P, FF], BF16)
+        nc.sync.dma_start(out=bias_fc1[:], in_=b_fc1.partition_broadcast(P))
+
+
+        h_words = h_rows[:].bitcast(F32)
+        h_grouped = tokens.tile([P, PASSES * T * PACK], BF16, tag="tok_b", align_bytes=64)
+        h_grouped_words = h_grouped[:].bitcast(F32).rearrange(
+            "p (g r u) -> p g r u", g=PASSES, u=2
+        )
+        h_codes = tokens.tile([P, PASSES * T], U32, tag="tok_codes", align_bytes=64)
+        h_scales = tokens.tile([P, PASSES * T], U8, tag="tok_scales", align_bytes=64)
+        for pair in range(TOK_TILES // 2):
+            for m in (2 * pair, 2 * pair + 1):
+                turned = psum.tile([P, PASSES, 2, P], F32, tag="turn", bufs=3)
+                for g in range(PASSES):
+                    for u in range(2):
+                        first_word = (D // 2) * m + (K_PASS // 2) * g
+                        nc.tensor.transpose(
+                            turned[:, g, u, :],
+                            h_words[:, first_word + u : first_word + K_PASS // 2 : 2],
+                            ident_f32[:],
+                        )
+                nc.scalar.copy(
+                    out=h_grouped_words[:, :, P * m : P * (m + 1), :],
+                    in_=turned[:].rearrange("p g u r -> p g r u"),
+                )
+            for g in range(PASSES):
+                first = T * g + 2 * P * pair
+                nc.vector.quantize_mx(
+                    out=h_codes[:, first : first + 2 * P].bitcast(FP8X4),
+                    scales=h_scales[:, first : first + 2 * P],
+                    in_=h_grouped[:, PACK * first : PACK * (first + 2 * P)],
+                )
+            if pair == 0:
+                transpose_vectors()
+
+        branch_t = [
+            tokens.tile([P, 4, T], F32, tag="tok_a", name="branch_t0"),
+            tokens.tile([P, 4, T], F32, tag="tok_b", name="branch_t1", align_bytes=64),
+        ]
+        for m0, count in TOKEN_GROUPS:
+            for c in range(D_CHUNKS):
+                acc = psum.tile([P, BANK], F32, tag="acc", bufs=5)
+                for g in range(PASSES):
+                    w_first = BLOCK * g + P * c
+                    t_first = T * g + P * m0
+                    nc.tensor.matmul_mx(
+                        out=acc[:, 0 : P * count],
+                        lhsT=block_codes[0][:, w_first : w_first + P].bitcast(FP8X4),
+                        lhsT_scale=block_scales[0][:, w_first : w_first + P],
+                        rhs=h_codes[:, t_first : t_first + P * count].bitcast(FP8X4),
+                        rhs_scale=h_scales[:, t_first : t_first + P * count],
+                        start=(g == 0),
+                        stop=(g == PASSES - 1),
+                    )
+                nc.scalar.activation(
+                    out=branch_t[c // 4][:, c % 4, P * m0 : P * (m0 + count)],
+                    in_=acc[:, 0 : P * count],
+                    func=ACT.Identity,
+                    scale=vec_cols[:, LS1 + c : LS1 + c + 1],
+                    bias=ls1_b[:, c : c + 1],
+                )
+        new_block_codes(4)
+        regroup_unit(4, nc.vector.tensor_copy)
+        regroup_unit(5, nc.vector.tensor_copy)
+        quantise_unit(4)
+        regroup_unit(6, nc.vector.tensor_copy)
+        quantise_unit(5)
+        regroup_unit(7, nc.vector.tensor_copy)
+        quantise_unit(6)
+        quantise_unit(7)
+
+        x_mid = const.tile([P, TOK_TILES, D], F32)
+        half_sums = const.tile([P, TOK_TILES, 2], F32)
+        neg_mean = const.tile([P, TOK_TILES], F32)
+        sum_sq = const.tile([P, TOK_TILES], F32)
+        var_eps = const.tile([P, TOK_TILES], F32)
+        rstd = const.tile([P, TOK_TILES], F32)
+        x_mid_view = out_0.rearrange("(p m) d -> p m d", p=P)
+        x_hat = []
+        for m in range(TOK_TILES):
+            for half in range(2):
+                branch = psum.tile([P, BANK], F32, tag="turn", bufs=3)
+                for q in range(4):
+                    nc.tensor.transpose(
+                        branch[:, P * q : P * (q + 1)],
+                        branch_t[half][:, q, P * m : P * (m + 1)],
+                        ident_f32[:],
+                    )
+                nc.vector.scalar_tensor_tensor(
+                    out=x_mid[:, m, BANK * half : BANK * (half + 1)],
+                    in0=branch[:],
+                    scalar=1.0,
+                    in1=x_rows[:, m, BANK * half : BANK * (half + 1)],
+                    op0=ALU.mult,
+                    op1=ALU.add,
+                    accum_out=half_sums[:, m, half : half + 1],
+                )
+            nc.sync.dma_start(out=x_mid_view[:, m, :], in_=x_mid[:, m, :])
+            nc.vector.tensor_scalar(
+                out=neg_mean[:, m : m + 1],
+                in0=half_sums[:, m, 0:1],
+                scalar1=half_sums[:, m, 1:2],
+                scalar2=-1.0 / D,
+                op0=ALU.add,
+                op1=ALU.mult,
+            )
+            normed = work.tile([P, D], F32, tag="f32", name="x_hat%d" % m)
+            nc.scalar.activation(
+                out=normed[:],
+                in_=x_mid[:, m, :],
+                func=ACT.Square,
+                bias=neg_mean[:, m : m + 1],
+                scale=1.0,
+                accum_out=sum_sq[:, m : m + 1],
+            )
+            nc.vector.tensor_scalar(
+                out=var_eps[:, m : m + 1],
+                in0=sum_sq[:, m : m + 1],
+                scalar1=1.0 / D,
+                scalar2=EPS,
+                op0=ALU.mult,
+                op1=ALU.add,
+            )
+            nc.gpsimd.tensor_tensor(
+                out=rstd[:, m : m + 1], in0=var_eps[:, m : m + 1], in1=neg_half[:], op=ALU.pow
+            )
+            nc.vector.tensor_scalar(
+                out=normed[:].rearrange("p (g t q) -> p g t q", g=PASSES, t=PACK),
+                in0=x_mid[:, m, :].rearrange("p (g q t) -> p g t q", g=PASSES, t=PACK),
+                scalar1=neg_mean[:, m : m + 1],
+                scalar2=rstd[:, m : m + 1],
+                op0=ALU.add,
+                op1=ALU.mult,
+            )
+            x_hat.append(normed)
+
+        h2_planes = tokens.tile([P, D_CHUNKS * T], BF16, tag="tok_a")
+        h2_grouped = tokens.tile([P, PASSES * T * PACK], BF16, tag="tok_b", align_bytes=64)
+        h2_codes = tokens.tile([P, PASSES * T], U32, tag="tok_codes", align_bytes=64)
+        h2_scales = tokens.tile([P, PASSES * T], U8, tag="tok_scales", align_bytes=64)
+        h2_chunks = h2_planes[:].rearrange("p (c r) -> p c r", c=D_CHUNKS)
+        for m0, count in TOKEN_GROUPS:
+            for c in range(D_CHUNKS):
+                turned = psum.tile([P, BANK], F32, tag="turn", bufs=3)
+                for i in range(count):
+                    nc.tensor.transpose(
+                        turned[:, P * i : P * (i + 1)],
+                        x_hat[m0 + i][:, P * c : P * (c + 1)],
+                        ident_f32[:],
+                    )
+                nc.scalar.activation(
+                    out=h2_chunks[:, c, P * m0 : P * (m0 + count)],
+                    in_=turned[:, 0 : P * count],
+                    func=ACT.Identity,
+                    scale=norm_cols[:, LN_G + c : LN_G + c + 1],
+                    bias=norm_cols[:, LN_B + c : LN_B + c + 1],
+                )
+            for g in range(PASSES):
+                first = T * g + P * m0
+                nc.vector.tensor_copy(
+                    out=h2_grouped[:, PACK * first : PACK * (first + P * count)].rearrange(
+                        "p (c i t) -> p c t i", i=4, t=PACK
+                    ),
+                    in_=h2_chunks[:, PACK * g : PACK * (g + 1), P * m0 : P * (m0 + count)].rearrange(
+                        "p t (c i) -> p c t i", i=4
+                    ),
+                )
+            for g in range(PASSES):
+                first = T * g + P * m0
+                nc.vector.quantize_mx(
+                    out=h2_codes[:, first : first + P * count].bitcast(FP8X4),
+                    scales=h2_scales[:, first : first + P * count],
+                    in_=h2_grouped[:, PACK * first : PACK * (first + P * count)],
+                )
+
+        for u in range(2 * UNITS_PER_BLOCK, 3 * UNITS_PER_BLOCK):
+            regroup_unit(u, nc.scalar.copy)
+        for u in range(2 * UNITS_PER_BLOCK, 3 * UNITS_PER_BLOCK):
+            quantise_unit(u)
+        for u in range(3 * UNITS_PER_BLOCK, FIRST_GPSIMD_UNIT):
+            regroup_unit(u, nc.vector.tensor_copy)
+        for u in range(3 * UNITS_PER_BLOCK, FIRST_GPSIMD_UNIT):
+            quantise_unit(u)
+
+        def regroup_on_gpsimd(u):
+            b, g, half = u // UNITS_PER_BLOCK, (u % UNITS_PER_BLOCK) // 2, u % 2
+            grouped = tokens.tile(
+                [P, BANK, PACK], BF16, tag="tok_b", name="grouped%d" % u, align_bytes=64
+            )
+            nc.gpsimd.tensor_scalar(
+                out=grouped[:],
+                in0=block_rows[b][:, g, :, BANK * half : BANK * (half + 1)].rearrange(
+                    "p t n -> p n t"
+                ),
+                scalar1=1.0,
+                scalar2=0.0,
+                op0=ALU.mult,
+                op1=ALU.add,
+            )
+            grouped_units[u] = grouped[:].rearrange("p n t -> p (n t)")
+
+        regroup_on_gpsimd(FIRST_GPSIMD_UNIT)
+        g_view = out_1.rearrange("(p m) f -> p m f", p=P)
+        units = UNITS_PER_BLOCK * (1 + FF_BLOCKS)
+        for b in range(1, 1 + FF_BLOCKS):
+            for m in range(TOK_TILES):
+                step = TOK_TILES * (b - 1) + m
+                hidden = work.tile([P, BLOCK], F32, tag="f32")
+                for half in range(BLOCK // BANK):
+                    acc = psum.tile([P, BANK], F32, tag="acc", bufs=5)
+                    for g in range(PASSES):
+                        t_first = T * g + P * m
+                        w_first = BLOCK * g + BANK * half
+                        nc.tensor.matmul_mx(
+                            out=acc[:],
+                            lhsT=h2_codes[:, t_first : t_first + P].bitcast(FP8X4),
+                            lhsT_scale=h2_scales[:, t_first : t_first + P],
+                            rhs=block_codes[b][:, w_first : w_first + BANK].bitcast(FP8X4),
+                            rhs_scale=block_scales[b][:, w_first : w_first + BANK],
+                            start=(g == 0),
+                            stop=(g == PASSES - 1),
+                        )
+                    ff_first = BLOCK * (b - 1) + BANK * half
+                    nc.vector.tensor_tensor(
+                        out=hidden[:, BANK * half : BANK * (half + 1)],
+                        in0=acc[:],
+                        in1=bias_fc1[:, ff_first : ff_first + BANK],
+                        op=ALU.add,
+                    )
+                u = FIRST_GPSIMD_UNIT + step // STEPS_PER_GPSIMD_UNIT
+                if step % STEPS_PER_GPSIMD_UNIT == STEPS_PER_GPSIMD_UNIT - 1 and u < units:
+                    quantise_unit(u)
+                    if u + 1 < units:
+                        regroup_on_gpsimd(u + 1)
+                nc.scalar.activation(out=hidden[:], in_=hidden[:], func=ACT.Gelu)
+                nc.sync.dma_start(out=g_view[:, m, BLOCK * (b - 1) : BLOCK * b], in_=hidden[:])

@@ -113,26 +113,29 @@ def tile_nestedtensorblock_pb_kernel(
         make_identity(nc, ident_f32[:])
         ident_bf16 = const.tile([P, P], BF16)
         nc.vector.tensor_copy(out=ident_bf16[:], in_=ident_f32[:])
-        neg_half = const.tile([P, 1], F32)
-        nc.vector.memset(neg_half[:], -0.5)
-        first_gelu = const.tile([P, 1], F32)
-        nc.scalar.activation(out=first_gelu[:], in_=neg_half[:], func=ACT.Gelu)
+        eps = const.tile([P, 1], F32)
+        nc.gpsimd.memset(eps[:], EPS)
+        first_call = const.tile([P, 1], F32)
+        nc.scalar.activation(out=first_call[:], in_=eps[:], func=ACT.Abs_reciprocal_sqrt)
 
         vec_cols = const.tile([P, 2 * D_CHUNKS], F32)
         norm_cols = const.tile([P, 2 * D_CHUNKS], F32)
         ls1_b = const.tile([P, D_CHUNKS], F32)
 
         def transpose_vectors():
-            vec_ps = psum.tile([P, P], BF16, tag="turn", bufs=3)
+            vec_ps = psum.tile([P, P], BF16, tag="acc", bufs=5)
             nc.tensor.transpose(vec_ps[:], vec_rows[:], ident_bf16[:])
             nc.vector.tensor_copy(out=vec_cols[:], in_=vec_ps[:, 0 : 2 * D_CHUNKS])
-            for i in range(2):
-                nc.vector.tensor_copy(
-                    out=norm_cols[:, D_CHUNKS * i : D_CHUNKS * (i + 1)],
-                    in_=norm_rows[i][:].rearrange("p g t -> p (g t)"),
-                )
+
             nc.vector.tensor_mul(
                 ls1_b[:], vec_cols[:, LS1 : LS1 + D_CHUNKS], vec_cols[:, B_PROJ : B_PROJ + D_CHUNKS]
+            )
+
+        transpose_vectors()
+        for i in range(2):
+            nc.gpsimd.tensor_copy(
+                out=norm_cols[:, D_CHUNKS * i : D_CHUNKS * (i + 1)],
+                in_=norm_rows[i][:].rearrange("p g t -> p (g t)"),
             )
 
         for b in range(4):
@@ -203,8 +206,6 @@ def tile_nestedtensorblock_pb_kernel(
                     scales=h_scales[:, first : first + 2 * P],
                     in_=h_grouped[:, PACK * first : PACK * (first + 2 * P)],
                 )
-            if pair == 0:
-                transpose_vectors()
 
         branch_t = [
             tokens.tile([P, 4, T], F32, tag="tok_a", name="branch_t0"),
@@ -246,7 +247,6 @@ def tile_nestedtensorblock_pb_kernel(
         half_sums = const.tile([P, TOK_TILES, 2], F32)
         neg_mean = const.tile([P, TOK_TILES], F32)
         sum_sq = const.tile([P, TOK_TILES], F32)
-        var_eps = const.tile([P, TOK_TILES], F32)
         rstd = const.tile([P, TOK_TILES], F32)
         x_mid_view = out_0.rearrange("(p m) d -> p m d", p=P)
         x_hat = []
@@ -286,20 +286,18 @@ def tile_nestedtensorblock_pb_kernel(
                 scale=1.0,
                 accum_out=sum_sq[:, m : m + 1],
             )
-            nc.vector.tensor_scalar(
-                out=var_eps[:, m : m + 1],
-                in0=sum_sq[:, m : m + 1],
-                scalar1=1.0 / D,
-                scalar2=EPS,
-                op0=ALU.mult,
-                op1=ALU.add,
+            nc.scalar.activation(
+                out=rstd[:, m : m + 1],
+                in_=sum_sq[:, m : m + 1],
+                func=ACT.Abs_reciprocal_sqrt,
+                bias=eps[:],
+                scale=1.0 / D,
             )
-            nc.gpsimd.tensor_tensor(
-                out=rstd[:, m : m + 1], in0=var_eps[:, m : m + 1], in1=neg_half[:], op=ALU.pow
-            )
+            if m == TOK_TILES - 1:
+                nc.scalar.activation(out=first_call[:], in_=rstd[:, m : m + 1], func=ACT.Gelu)
             nc.vector.tensor_scalar(
-                out=normed[:].rearrange("p (g t q) -> p g t q", g=PASSES, t=PACK),
-                in0=x_mid[:, m, :].rearrange("p (g q t) -> p g t q", g=PASSES, t=PACK),
+                out=normed[:].rearrange("p (g t q) -> p g q t", g=PASSES, t=PACK),
+                in0=x_mid[:, m, :].rearrange("p (g q t) -> p g q t", g=PASSES, t=PACK),
                 scalar1=neg_mean[:, m : m + 1],
                 scalar2=rstd[:, m : m + 1],
                 op0=ALU.add,

@@ -23,8 +23,9 @@ BLOCK = 2 * BANK
 FF_BLOCKS = FF // BLOCK
 UNITS_PER_BLOCK = PASSES * (BLOCK // BANK)
 TOKEN_GROUPS = ((0, 4), (4, 2))
-FIRST_GPSIMD_UNIT = 3 * UNITS_PER_BLOCK + 2
-STEPS_PER_GPSIMD_UNIT = 3
+FIRST_GPSIMD_UNIT = 3 * UNITS_PER_BLOCK
+GPSIMD_UNITS = 6
+FIRST_LATE_SCALAR_UNIT = FIRST_GPSIMD_UNIT + GPSIMD_UNITS
 EPS = 1e-5
 FLOPS = 2 * T * D * (D + FF)
 
@@ -76,14 +77,14 @@ def tile_nestedtensorblock_pb_kernel(
                 [P, PASSES * BLOCK], U8, tag="w_scales", name="w_scales%d" % b, align_bytes=64
             )
 
-        new_block_rows(0)
+        wp_units = weights.tile([P, UNITS_PER_BLOCK, PACK, BANK], BF16, tag="w_rows", name="wp_units")
         wp_view = w_proj.rearrange("(g p t) n -> p g t n", g=PASSES, t=PACK)
-        for g in range(PASSES):
-            for u in range(2):
-                nc.sync.dma_start(
-                    out=block_rows[0][:, g, 2 * u : 2 * u + 2, :],
-                    in_=wp_view[:, g, 2 * u : 2 * u + 2, :],
-                )
+        for u in range(UNITS_PER_BLOCK):
+            half = u % 2
+            nc.sync.dma_start(
+                out=wp_units[:, u, :, :],
+                in_=wp_view[:, u // 2, :, BANK * half : BANK * (half + 1)],
+            )
 
         h_rows = tokens.tile([P, TOK_TILES * D], BF16, tag="tok_a")
         h_view = h_attn.rearrange("(p m) d -> p m d", p=P)
@@ -144,14 +145,16 @@ def tile_nestedtensorblock_pb_kernel(
 
         def regroup_unit(u, copy):
             b, g, half = u // UNITS_PER_BLOCK, (u % UNITS_PER_BLOCK) // 2, u % 2
+            if b == 0:
+                rows = wp_units[:, u, :, :]
+            else:
+                rows = block_rows[b][:, g, :, BANK * half : BANK * (half + 1)]
             grouped = stage.tile(
                 [P, BANK * PACK], BF16, tag="grouped", name="grouped%d" % u, align_bytes=64
             )
             copy(
                 out=grouped[:].rearrange("p (c i t) -> p c t i", i=4, t=PACK),
-                in_=block_rows[b][:, g, :, BANK * half : BANK * (half + 1)].rearrange(
-                    "p t (c i) -> p c t i", i=4
-                ),
+                in_=rows.rearrange("p t (c i) -> p c t i", i=4),
             )
             grouped_units[u] = grouped[:]
 
@@ -345,12 +348,8 @@ def tile_nestedtensorblock_pb_kernel(
                 )
 
         for u in range(2 * UNITS_PER_BLOCK, 3 * UNITS_PER_BLOCK):
-            regroup_unit(u, nc.scalar.copy)
+            regroup_unit(u, nc.scalar.copy if u % UNITS_PER_BLOCK < 2 else nc.vector.tensor_copy)
         for u in range(2 * UNITS_PER_BLOCK, 3 * UNITS_PER_BLOCK):
-            quantise_unit(u)
-        for u in range(3 * UNITS_PER_BLOCK, FIRST_GPSIMD_UNIT):
-            regroup_unit(u, nc.vector.tensor_copy)
-        for u in range(3 * UNITS_PER_BLOCK, FIRST_GPSIMD_UNIT):
             quantise_unit(u)
 
         def regroup_on_gpsimd(u):
@@ -372,36 +371,42 @@ def tile_nestedtensorblock_pb_kernel(
 
         regroup_on_gpsimd(FIRST_GPSIMD_UNIT)
         g_view = out_1.rearrange("(p m) f -> p m f", p=P)
-        units = UNITS_PER_BLOCK * (1 + FF_BLOCKS)
-        for b in range(1, 1 + FF_BLOCKS):
-            for m in range(TOK_TILES):
-                step = TOK_TILES * (b - 1) + m
-                hidden = work.tile([P, BLOCK], F32, tag="f32")
-                for half in range(BLOCK // BANK):
-                    acc = psum.tile([P, BANK], F32, tag="acc", bufs=5)
-                    for g in range(PASSES):
-                        t_first = T * g + P * m
-                        w_first = BLOCK * g + BANK * half
-                        nc.tensor.matmul_mx(
-                            out=acc[:],
-                            lhsT=h2_codes[:, t_first : t_first + P].bitcast(FP8X4),
-                            lhsT_scale=h2_scales[:, t_first : t_first + P],
-                            rhs=block_codes[b][:, w_first : w_first + BANK].bitcast(FP8X4),
-                            rhs_scale=block_scales[b][:, w_first : w_first + BANK],
-                            start=(g == 0),
-                            stop=(g == PASSES - 1),
+        last_step = {(5 * (i + 1)) // 2 - 1: FIRST_GPSIMD_UNIT + i for i in range(GPSIMD_UNITS)}
+        scalar_step = {3: FIRST_LATE_SCALAR_UNIT, 7: FIRST_LATE_SCALAR_UNIT + 1}
+        with tc.manual_schedule(engines={mybir.EngineType.Activation}):
+            for b in range(1, 1 + FF_BLOCKS):
+                for m in range(TOK_TILES):
+                    step = TOK_TILES * (b - 1) + m
+                    hidden = work.tile([P, BLOCK], F32, tag="f32")
+                    for half in range(BLOCK // BANK):
+                        acc = psum.tile([P, BANK], F32, tag="acc", bufs=5)
+                        for g in range(PASSES):
+                            t_first = T * g + P * m
+                            w_first = BLOCK * g + BANK * half
+                            nc.tensor.matmul_mx(
+                                out=acc[:],
+                                lhsT=h2_codes[:, t_first : t_first + P].bitcast(FP8X4),
+                                lhsT_scale=h2_scales[:, t_first : t_first + P],
+                                rhs=block_codes[b][:, w_first : w_first + BANK].bitcast(FP8X4),
+                                rhs_scale=block_scales[b][:, w_first : w_first + BANK],
+                                start=(g == 0),
+                                stop=(g == PASSES - 1),
+                            )
+                        ff_first = BLOCK * (b - 1) + BANK * half
+                        nc.vector.tensor_tensor(
+                            out=hidden[:, BANK * half : BANK * (half + 1)],
+                            in0=acc[:],
+                            in1=bias_fc1[:, ff_first : ff_first + BANK],
+                            op=ALU.add,
                         )
-                    ff_first = BLOCK * (b - 1) + BANK * half
-                    nc.vector.tensor_tensor(
-                        out=hidden[:, BANK * half : BANK * (half + 1)],
-                        in0=acc[:],
-                        in1=bias_fc1[:, ff_first : ff_first + BANK],
-                        op=ALU.add,
-                    )
-                u = FIRST_GPSIMD_UNIT + step // STEPS_PER_GPSIMD_UNIT
-                if step % STEPS_PER_GPSIMD_UNIT == STEPS_PER_GPSIMD_UNIT - 1 and u < units:
-                    quantise_unit(u)
-                    if u + 1 < units:
-                        regroup_on_gpsimd(u + 1)
-                nc.scalar.activation(out=hidden[:], in_=hidden[:], func=ACT.Gelu)
-                nc.sync.dma_start(out=g_view[:, m, BLOCK * (b - 1) : BLOCK * b], in_=hidden[:])
+                    if step in last_step:
+                        u = last_step[step]
+                        quantise_unit(u)
+                        if u + 1 < FIRST_LATE_SCALAR_UNIT:
+                            regroup_on_gpsimd(u + 1)
+                    nc.scalar.activation(out=hidden[:], in_=hidden[:], func=ACT.Gelu)
+                    if step in scalar_step:
+                        regroup_unit(scalar_step[step], nc.scalar.copy)
+                    if step - 4 in scalar_step:
+                        quantise_unit(scalar_step[step - 4])
+                    nc.sync.dma_start(out=g_view[:, m, BLOCK * (b - 1) : BLOCK * b], in_=hidden[:])

@@ -23,8 +23,9 @@ BLOCK = 2 * BANK
 FF_BLOCKS = FF // BLOCK
 UNITS_PER_BLOCK = PASSES * (BLOCK // BANK)
 TOKEN_GROUPS = ((0, 4), (4, 2))
-FIRST_GPSIMD_UNIT = 3 * UNITS_PER_BLOCK
-GPSIMD_UNITS = 6
+FIRST_GPSIMD_UNIT = 3 * UNITS_PER_BLOCK + 1
+GPSIMD_UNITS = 5
+STEPS_PER_GPSIMD_UNIT = 3
 FIRST_LATE_SCALAR_UNIT = FIRST_GPSIMD_UNIT + GPSIMD_UNITS
 EPS = 1e-5
 FLOPS = 2 * T * D * (D + FF)
@@ -352,6 +353,9 @@ def tile_nestedtensorblock_pb_kernel(
         for u in range(2 * UNITS_PER_BLOCK, 3 * UNITS_PER_BLOCK):
             quantise_unit(u)
 
+        regroup_unit(3 * UNITS_PER_BLOCK, nc.vector.tensor_copy)
+        quantise_unit(3 * UNITS_PER_BLOCK)
+
         def regroup_on_gpsimd(u):
             b, g, half = u // UNITS_PER_BLOCK, (u % UNITS_PER_BLOCK) // 2, u % 2
             grouped = tokens.tile(
@@ -371,8 +375,11 @@ def tile_nestedtensorblock_pb_kernel(
 
         regroup_on_gpsimd(FIRST_GPSIMD_UNIT)
         g_view = out_1.rearrange("(p m) f -> p m f", p=P)
-        last_step = {(5 * (i + 1)) // 2 - 1: FIRST_GPSIMD_UNIT + i for i in range(GPSIMD_UNITS)}
-        scalar_step = {3: FIRST_LATE_SCALAR_UNIT, 7: FIRST_LATE_SCALAR_UNIT + 1}
+        last_step = {
+            STEPS_PER_GPSIMD_UNIT * (i + 1) - 1: FIRST_GPSIMD_UNIT + i for i in range(GPSIMD_UNITS)
+        }
+        scalar_step = {4: FIRST_LATE_SCALAR_UNIT, 9: FIRST_LATE_SCALAR_UNIT + 1}
+        quantise_step = {8: FIRST_LATE_SCALAR_UNIT, 14: FIRST_LATE_SCALAR_UNIT + 1}
         with tc.manual_schedule(engines={mybir.EngineType.Activation}):
             for b in range(1, 1 + FF_BLOCKS):
                 for m in range(TOK_TILES):
@@ -399,6 +406,8 @@ def tile_nestedtensorblock_pb_kernel(
                             in1=bias_fc1[:, ff_first : ff_first + BANK],
                             op=ALU.add,
                         )
+                    if step in quantise_step:
+                        quantise_unit(quantise_step[step])
                     if step in last_step:
                         u = last_step[step]
                         quantise_unit(u)
@@ -407,6 +416,4 @@ def tile_nestedtensorblock_pb_kernel(
                     nc.scalar.activation(out=hidden[:], in_=hidden[:], func=ACT.Gelu)
                     if step in scalar_step:
                         regroup_unit(scalar_step[step], nc.scalar.copy)
-                    if step - 4 in scalar_step:
-                        quantise_unit(scalar_step[step - 4])
                     nc.sync.dma_start(out=g_view[:, m, BLOCK * (b - 1) : BLOCK * b], in_=hidden[:])

from contextlib import ExitStack

import concourse.mybir as mybir
from concourse.masks import make_identity

F32 = mybir.dt.float32
BF16 = mybir.dt.bfloat16
U32 = mybir.dt.uint32
U8 = mybir.dt.uint8
FP8X4 = mybir.dt.float8_e4m3fn_x4
ACT = mybir.ActivationFunctionType
ALU = mybir.AluOpType

P = 128
PACK = 4
K_PASS = P * PACK
T, D, FF = 768, 1024, 4096
PASSES = D // K_PASS
TOK_TILES = T // P
D_CHUNKS = D // P
BANK = 512
BLOCK = 2 * BANK
FF_BLOCKS = FF // BLOCK
UNITS_PER_BLOCK = PASSES * (BLOCK // BANK)
TOKEN_GROUPS = ((0, 4), (4, 2))
FIRST_GPSIMD_UNIT = 3 * UNITS_PER_BLOCK + 1
GPSIMD_UNITS = 5
STEPS_PER_GPSIMD_UNIT = 3
FIRST_LATE_SCALAR_UNIT = FIRST_GPSIMD_UNIT + GPSIMD_UNITS
EPS = 1e-5
FLOPS = 2 * T * D * (D + FF)

B_PROJ, LS1 = 0, D_CHUNKS
LN_G, LN_B = 0, D_CHUNKS


def tile_nestedtensorblock_pb_kernel(
    tc, h_attn, x, w_proj, b_proj, ls1, ln2_g, ln2_b, w_fc1, b_fc1, out_0, out_1
):
    nc = tc.nc
    with ExitStack() as ctx:
        const = ctx.enter_context(tc.tile_pool(name="const", bufs=1))
        tokens = ctx.enter_context(tc.tile_pool(name="tokens", bufs=1))
        weights = ctx.enter_context(tc.tile_pool(name="weights", bufs=4))
        stage = ctx.enter_context(tc.tile_pool(name="stage", bufs=4))
        work = ctx.enter_context(tc.tile_pool(name="work", bufs=8))
        psum = ctx.enter_context(tc.psum_pool(name="psum", bufs=1))

        vec_rows = const.tile([P, P], BF16)
        nc.vector.memset(vec_rows[:], 0.0)
        for first_row, vec in ((B_PROJ, b_proj), (LS1, ls1)):
            nc.scalar.dma_start(
                out=vec_rows[first_row : first_row + D_CHUNKS, :],
                in_=vec.rearrange("(r c) -> r c", c=P),
            )
        norm_rows = []
        for i, vec in ((0, ln2_g), (1, ln2_b)):
            rows = const.tile([P, PASSES, PACK], BF16, name="norm_rows%d" % i)
            nc.scalar.dma_start(
                out=rows[:], in_=vec.rearrange("(g p t) -> p g t", g=PASSES, t=PACK)
            )
            norm_rows.append(rows)

        block_rows = {}
        block_codes = {}
        block_scales = {}

        def new_block_rows(b):
            block_rows[b] = weights.tile(
                [P, PASSES, PACK, BLOCK], BF16, tag="w_rows", name="w_rows%d" % b
            )

        def new_block_codes(b):
            block_codes[b] = weights.tile(
                [P, PASSES * BLOCK], U32, tag="w_codes", name="w_codes%d" % b, align_bytes=64
            )
            block_scales[b] = weights.tile(
                [P, PASSES * BLOCK], U8, tag="w_scales", name="w_scales%d" % b, align_bytes=64
            )

        wp_units = weights.tile([P, UNITS_PER_BLOCK, PACK, BANK], BF16, tag="w_rows", name="wp_units")
        wp_view = w_proj.rearrange("(g p t) n -> p g t n", g=PASSES, t=PACK)
        for u in range(UNITS_PER_BLOCK):
            half = u % 2
            nc.sync.dma_start(
                out=wp_units[:, u, :, :],
                in_=wp_view[:, u // 2, :, BANK * half : BANK * (half + 1)],
            )

        h_rows = tokens.tile([P, TOK_TILES * D], BF16, tag="tok_a")
        h_view = h_attn.rearrange("(p m) d -> p m d", p=P)
        for pair in range(TOK_TILES // 2):
            nc.sync.dma_start(
                out=h_rows[:, 2 * D * pair : 2 * D * (pair + 1)].rearrange("p (m d) -> p m d", m=2),
                in_=h_view[:, 2 * pair : 2 * pair + 2, :],
            )

        wf_view = w_fc1.rearrange("(g p t) n -> p g t n", g=PASSES, t=PACK)

        def load_ff_block(b):
            new_block_rows(b)
            for g in range(PASSES):
                nc.sync.dma_start(
                    out=block_rows[b][:, g, :, :],
                    in_=wf_view[:, g, :, BLOCK * (b - 1) : BLOCK * b],
                )

        load_ff_block(1)
        x_rows = const.tile([P, TOK_TILES, D], BF16)
        nc.sync.dma_start(out=x_rows[:], in_=x.rearrange("(p m) d -> p m d", p=P))
        load_ff_block(2)
        load_ff_block(3)

        ident_f32 = const.tile([P, P], F32)
        make_identity(nc, ident_f32[:])
        ident_bf16 = const.tile([P, P], BF16)
        nc.vector.tensor_copy(out=ident_bf16[:], in_=ident_f32[:])
        eps = const.tile([P, 1], F32)
        nc.gpsimd.memset(eps[:], EPS)
        first_call = const.tile([P, 1], F32)
        nc.scalar.activation(out=first_call[:], in_=eps[:], func=ACT.Abs_reciprocal_sqrt)

        vec_cols = const.tile([P, 2 * D_CHUNKS], F32)
        norm_cols = const.tile([P, 2 * D_CHUNKS], F32)
        ls1_b = const.tile([P, D_CHUNKS], F32)

        def transpose_vectors():
            vec_ps = psum.tile([P, P], BF16, tag="acc", bufs=5)
            nc.tensor.transpose(vec_ps[:], vec_rows[:], ident_bf16[:])
            nc.vector.tensor_copy(out=vec_cols[:], in_=vec_ps[:, 0 : 2 * D_CHUNKS])

            nc.vector.tensor_mul(
                ls1_b[:], vec_cols[:, LS1 : LS1 + D_CHUNKS], vec_cols[:, B_PROJ : B_PROJ + D_CHUNKS]
            )

        transpose_vectors()
        for i in range(2):
            nc.gpsimd.tensor_copy(
                out=norm_cols[:, D_CHUNKS * i : D_CHUNKS * (i + 1)],
                in_=norm_rows[i][:].rearrange("p g t -> p (g t)"),
            )

        for b in range(4):
            new_block_codes(b)
        grouped_units = {}

        def regroup_unit(u, copy):
            b, g, half = u // UNITS_PER_BLOCK, (u % UNITS_PER_BLOCK) // 2, u % 2
            if b == 0:
                rows = wp_units[:, u, :, :]
            else:
                rows = block_rows[b][:, g, :, BANK * half : BANK * (half + 1)]
            grouped = stage.tile(
                [P, BANK * PACK], BF16, tag="grouped", name="grouped%d" % u, align_bytes=64
            )
            copy(
                out=grouped[:].rearrange("p (c i t) -> p c t i", i=4, t=PACK),
                in_=rows.rearrange("p t (c i) -> p c t i", i=4),
            )
            grouped_units[u] = grouped[:]

        def quantise_unit(u):
            b, g, half = u // UNITS_PER_BLOCK, (u % UNITS_PER_BLOCK) // 2, u % 2
            first = BLOCK * g + BANK * half
            nc.vector.quantize_mx(
                out=block_codes[b][:, first : first + BANK].bitcast(FP8X4),
                scales=block_scales[b][:, first : first + BANK],
                in_=grouped_units[u],
            )

        regroup_unit(0, nc.vector.tensor_copy)
        regroup_unit(1, nc.scalar.copy)
        quantise_unit(0)
        regroup_unit(2, nc.vector.tensor_copy)
        regroup_unit(3, nc.scalar.copy)
        quantise_unit(1)
        quantise_unit(2)
        quantise_unit(3)
        load_ff_block(4)
        bias_fc1 = const.tile([P, FF], BF16)
        nc.sync.dma_start(out=bias_fc1[:], in_=b_fc1.partition_broadcast(P))


        h_words = h_rows[:].bitcast(F32)
        h_grouped = tokens.tile([P, PASSES * T * PACK], BF16, tag="tok_b", align_bytes=64)
        h_grouped_words = h_grouped[:].bitcast(F32).rearrange(
            "p (g r u) -> p g r u", g=PASSES, u=2
        )
        h_codes = tokens.tile([P, PASSES * T], U32, tag="tok_codes", align_bytes=64)
        h_scales = tokens.tile([P, PASSES * T], U8, tag="tok_scales", align_bytes=64)
        for pair in range(TOK_TILES // 2):
            for m in (2 * pair, 2 * pair + 1):
                turned = psum.tile([P, PASSES, 2, P], F32, tag="turn", bufs=3)
                for g in range(PASSES):
                    for u in range(2):
                        first_word = (D // 2) * m + (K_PASS // 2) * g
                        nc.tensor.transpose(
                            turned[:, g, u, :],
                            h_words[:, first_word + u : first_word + K_PASS // 2 : 2],
                            ident_f32[:],
                        )
                nc.scalar.copy(
                    out=h_grouped_words[:, :, P * m : P * (m + 1), :],
                    in_=turned[:].rearrange("p g u r -> p g r u"),
                )
            for g in range(PASSES):
                first = T * g + 2 * P * pair
                nc.vector.quantize_mx(
                    out=h_codes[:, first : first + 2 * P].bitcast(FP8X4),
                    scales=h_scales[:, first : first + 2 * P],
                    in_=h_grouped[:, PACK * first : PACK * (first + 2 * P)],
                )

        branch_t = [
            tokens.tile([P, 4, T], F32, tag="tok_a", name="branch_t0"),
            tokens.tile([P, 4, T], F32, tag="tok_b", name="branch_t1", align_bytes=64),
        ]
        for m0, count in TOKEN_GROUPS:
            for c in range(D_CHUNKS):
                acc = psum.tile([P, BANK], F32, tag="acc", bufs=5)
                for g in range(PASSES):
                    w_first = BLOCK * g + P * c
                    t_first = T * g + P * m0
                    nc.tensor.matmul_mx(
                        out=acc[:, 0 : P * count],
                        lhsT=block_codes[0][:, w_first : w_first + P].bitcast(FP8X4),
                        lhsT_scale=block_scales[0][:, w_first : w_first + P],
                        rhs=h_codes[:, t_first : t_first + P * count].bitcast(FP8X4),
                        rhs_scale=h_scales[:, t_first : t_first + P * count],
                        start=(g == 0),
                        stop=(g == PASSES - 1),
                    )
                nc.scalar.activation(
                    out=branch_t[c // 4][:, c % 4, P * m0 : P * (m0 + count)],
                    in_=acc[:, 0 : P * count],
                    func=ACT.Identity,
                    scale=vec_cols[:, LS1 + c : LS1 + c + 1],
                    bias=ls1_b[:, c : c + 1],
                )
        new_block_codes(4)
        regroup_unit(4, nc.vector.tensor_copy)
        regroup_unit(5, nc.vector.tensor_copy)
        quantise_unit(4)
        regroup_unit(6, nc.vector.tensor_copy)
        quantise_unit(5)
        regroup_unit(7, nc.vector.tensor_copy)
        quantise_unit(6)
        quantise_unit(7)

        x_mid = const.tile([P, TOK_TILES, D], F32)
        half_sums = const.tile([P, TOK_TILES, 2], F32)
        neg_mean = const.tile([P, TOK_TILES], F32)
        sum_sq = const.tile([P, TOK_TILES], F32)
        rstd = const.tile([P, TOK_TILES], F32)
        x_mid_view = out_0.rearrange("(p m) d -> p m d", p=P)
        x_hat = []
        for m in range(TOK_TILES):
            for half in range(2):
                branch = psum.tile([P, BANK], F32, tag="turn", bufs=3)
                for q in range(4):
                    nc.tensor.transpose(
                        branch[:, P * q : P * (q + 1)],
                        branch_t[half][:, q, P * m : P * (m + 1)],
                        ident_f32[:],
                    )
                nc.vector.scalar_tensor_tensor(
                    out=x_mid[:, m, BANK * half : BANK * (half + 1)],
                    in0=branch[:],
                    scalar=1.0,
                    in1=x_rows[:, m, BANK * half : BANK * (half + 1)],
                    op0=ALU.mult,
                    op1=ALU.add,
                    accum_out=half_sums[:, m, half : half + 1],
                )
            nc.sync.dma_start(out=x_mid_view[:, m, :], in_=x_mid[:, m, :])
            nc.vector.tensor_scalar(
                out=neg_mean[:, m : m + 1],
                in0=half_sums[:, m, 0:1],
                scalar1=half_sums[:, m, 1:2],
                scalar2=-1.0 / D,
                op0=ALU.add,
                op1=ALU.mult,
            )
            normed = work.tile([P, D], F32, tag="f32", name="x_hat%d" % m)
            nc.scalar.activation(
                out=normed[:],
                in_=x_mid[:, m, :],
                func=ACT.Square,
                bias=neg_mean[:, m : m + 1],
                scale=1.0,
                accum_out=sum_sq[:, m : m + 1],
            )
            nc.scalar.activation(
                out=rstd[:, m : m + 1],
                in_=sum_sq[:, m : m + 1],
                func=ACT.Abs_reciprocal_sqrt,
                bias=eps[:],
                scale=1.0 / D,
            )
            if m == TOK_TILES - 1:
                nc.scalar.activation(out=first_call[:], in_=rstd[:, m : m + 1], func=ACT.Gelu)
            nc.vector.tensor_scalar(
                out=normed[:].rearrange("p (g t q) -> p g q t", g=PASSES, t=PACK),
                in0=x_mid[:, m, :].rearrange("p (g q t) -> p g q t", g=PASSES, t=PACK),
                scalar1=neg_mean[:, m : m + 1],
                scalar2=rstd[:, m : m + 1],
                op0=ALU.add,
                op1=ALU.mult,
            )
            x_hat.append(normed)

        h2_planes = tokens.tile([P, D_CHUNKS * T], BF16, tag="tok_a")
        h2_grouped = tokens.tile([P, PASSES * T * PACK], BF16, tag="tok_b", align_bytes=64)
        h2_codes = tokens.tile([P, PASSES * T], U32, tag="tok_codes", align_bytes=64)
        h2_scales = tokens.tile([P, PASSES * T], U8, tag="tok_scales", align_bytes=64)
        h2_chunks = h2_planes[:].rearrange("p (c r) -> p c r", c=D_CHUNKS)
        for m0, count in TOKEN_GROUPS:
            for c in range(D_CHUNKS):
                turned = psum.tile([P, BANK], F32, tag="turn", bufs=3)
                for i in range(count):
                    nc.tensor.transpose(
                        turned[:, P * i : P * (i + 1)],
                        x_hat[m0 + i][:, P * c : P * (c + 1)],
                        ident_f32[:],
                    )
                nc.scalar.activation(
                    out=h2_chunks[:, c, P * m0 : P * (m0 + count)],
                    in_=turned[:, 0 : P * count],
                    func=ACT.Identity,
                    scale=norm_cols[:, LN_G + c : LN_G + c + 1],
                    bias=norm_cols[:, LN_B + c : LN_B + c + 1],
                )
            for g in range(PASSES):
                first = T * g + P * m0
                nc.vector.tensor_copy(
                    out=h2_grouped[:, PACK * first : PACK * (first + P * count)].rearrange(
                        "p (c i t) -> p c t i", i=4, t=PACK
                    ),
                    in_=h2_chunks[:, PACK * g : PACK * (g + 1), P * m0 : P * (m0 + count)].rearrange(
                        "p t (c i) -> p c t i", i=4
                    ),
                )
            for g in range(PASSES):
                first = T * g + P * m0
                nc.vector.quantize_mx(
                    out=h2_codes[:, first : first + P * count].bitcast(FP8X4),
                    scales=h2_scales[:, first : first + P * count],
                    in_=h2_grouped[:, PACK * first : PACK * (first + P * count)],
                )

        for u in range(2 * UNITS_PER_BLOCK, 3 * UNITS_PER_BLOCK):
            regroup_unit(u, nc.scalar.copy if u % UNITS_PER_BLOCK < 2 else nc.vector.tensor_copy)
        for u in range(2 * UNITS_PER_BLOCK, 3 * UNITS_PER_BLOCK):
            quantise_unit(u)

        regroup_unit(3 * UNITS_PER_BLOCK, nc.vector.tensor_copy)
        quantise_unit(3 * UNITS_PER_BLOCK)

        def regroup_on_gpsimd(u):
            b, g, half = u // UNITS_PER_BLOCK, (u % UNITS_PER_BLOCK) // 2, u % 2
            grouped = tokens.tile(
                [P, BANK, PACK], BF16, tag="tok_b", name="grouped%d" % u, align_bytes=64
            )
            nc.gpsimd.tensor_scalar(
                out=grouped[:],
                in0=block_rows[b][:, g, :, BANK * half : BANK * (half + 1)].rearrange(
                    "p t n -> p n t"
                ),
                scalar1=1.0,
                scalar2=0.0,
                op0=ALU.mult,
                op1=ALU.add,
            )
            grouped_units[u] = grouped[:].rearrange("p n t -> p (n t)")

        regroup_on_gpsimd(FIRST_GPSIMD_UNIT)
        g_view = out_1.rearrange("(p m) f -> p m f", p=P)
        last_step = {
            STEPS_PER_GPSIMD_UNIT * (i + 1) - 1: FIRST_GPSIMD_UNIT + i for i in range(GPSIMD_UNITS)
        }
        scalar_step = {4: FIRST_LATE_SCALAR_UNIT, 9: FIRST_LATE_SCALAR_UNIT + 1}
        quantise_step = {8: FIRST_LATE_SCALAR_UNIT, 14: FIRST_LATE_SCALAR_UNIT + 1}
        with tc.manual_schedule(engines={mybir.EngineType.Activation}):
            for b in range(1, 1 + FF_BLOCKS):
                for m in range(TOK_TILES):
                    step = TOK_TILES * (b - 1) + m
                    hidden = work.tile([P, BLOCK], F32, tag="f32")
                    for half in range(BLOCK // BANK):
                        acc = psum.tile([P, BANK], F32, tag="acc", bufs=5)
                        for g in range(PASSES):
                            t_first = T * g + P * m
                            w_first = BLOCK * g + BANK * half
                            nc.tensor.matmul_mx(
                                out=acc[:],
                                lhsT=h2_codes[:, t_first : t_first + P].bitcast(FP8X4),
                                lhsT_scale=h2_scales[:, t_first : t_first + P],
                                rhs=block_codes[b][:, w_first : w_first + BANK].bitcast(FP8X4),
                                rhs_scale=block_scales[b][:, w_first : w_first + BANK],
                                start=(g == 0),
                                stop=(g == PASSES - 1),
                            )
                        ff_first = BLOCK * (b - 1) + BANK * half
                        nc.vector.tensor_tensor(
                            out=hidden[:, BANK * half : BANK * (half + 1)],
                            in0=acc[:],
                            in1=bias_fc1[:, ff_first : ff_first + BANK],
                            op=ALU.add,
                        )
                    if step in quantise_step:
                        quantise_unit(quantise_step[step])
                    if step in last_step:
                        u = last_step[step]
                        quantise_unit(u)
                        if u + 1 < FIRST_LATE_SCALAR_UNIT:
                            regroup_on_gpsimd(u + 1)
                    nc.scalar.activation(out=hidden[:], in_=hidden[:], func=ACT.Gelu)
                    if step in scalar_step:
                        regroup_unit(scalar_step[step], nc.scalar.copy)
                    nc.sync.dma_start(out=g_view[:, m, BLOCK * (b - 1) : BLOCK * b], in_=hidden[:])
